import numpy as np
import ml_dtypes


def mxq(x, axis, fmt="e4m3"):
    dtype, down = {"e4m3": (ml_dtypes.float8_e4m3fn, 7), "e5m2": (ml_dtypes.float8_e5m2, 14)}[fmt]
    v = np.moveaxis(np.asarray(x, np.float32).astype(ml_dtypes.bfloat16).astype(np.float64), axis, -1)
    blocks = v.reshape(v.shape[:-1] + (-1, 32))
    amax = np.abs(blocks).max(-1, keepdims=True)
    byte = np.maximum(np.where(amax > 0, np.frexp(amax)[1] - 1 + 127, 0) - down, 1)
    scale = np.exp2(byte - 127.0)
    codes = (blocks / scale).astype(np.float32).astype(dtype).astype(np.float64)
    return np.moveaxis((codes * scale).reshape(v.shape), -1, axis)


WIDE = False


def mx_kscale(k):
    if not WIDE:
        return np.ones(k)
    levels = np.array([10, -10, 5, -5, 0])
    a = np.random.permutation(np.resize(levels, k // 512 * 4)).reshape(k // 512, 4)
    idx = np.arange(k)
    return np.exp2(a[idx // 512, idx % 128 // 32])


BF16 = ml_dtypes.bfloat16


def bf(x):
    return np.asarray(x, np.float32).astype(BF16)


def f64(x):
    return np.asarray(x).astype(np.float64)


B, C, D, R, STEPS = 128, 1024, 1024, 4, 5
EPS = 1e-8


def shared_mix(n, u):
    return sum(np.random.standard_normal((n, 1)) * u[r] for r in range(R))


def setup_inputs():
    u = np.random.standard_normal((R, D)) / np.sqrt(R)
    s = mx_kscale(D)
    r = (s / s.max())[np.arange(B) * D // B][:, None]
    current = (0.6 * shared_mix(B, u) + 0.45 * np.random.standard_normal((B, D))) * r
    memory = 2.4 * shared_mix(C, u) + 1.8 * np.random.standard_normal((C, D))
    return {"current": bf(current), "memory_matrix": bf(memory)}


def reference(current, memory_matrix):
    cur, mem = f64(current), f64(memory_matrix)
    mem_norm = np.maximum(np.sqrt((mem * mem).sum(-1)), EPS)
    cur_norm = np.maximum(np.sqrt((cur * cur).sum(-1, keepdims=True)), EPS)
    sim = (mxq(cur, 1, "e4m3") @ mxq(mem, 1, "e4m3").T) / (cur_norm * mem_norm[None, :])
    e = np.exp(sim - sim.max(-1, keepdims=True))
    attracted = (mxq(e, 1, "e4m3") @ mxq(mem, 0, "e4m3")) / e.sum(-1, keepdims=True)
    return 0.8 * attracted + 0.2 * cur

@@ -1,0 +1,251 @@
+from contextlib import ExitStack
+
+import concourse.mybir as mybir
+from concourse.masks import make_identity
+
+F32 = mybir.dt.float32
+BF16 = mybir.dt.bfloat16
+U32 = mybir.dt.uint32
+U8 = mybir.dt.uint8
+FP8X4 = mybir.dt.float8_e4m3fn_x4
+ACT = mybir.ActivationFunctionType
+ALU = mybir.AluOpType
+AXIS_X = mybir.AxisListType.X
+
+P = 128
+ROWS = 1024
+FEATURES = 1024
+PACK = 4
+K_PASS = P * PACK
+PASSES = 2
+ROW_TILES = ROWS // P
+CHUNK_TILES = 2
+CHUNKS = ROW_TILES // CHUNK_TILES
+HALF_CHUNKS = CHUNKS // PASSES
+WORD_BLOCKS = FEATURES // 2 // P
+N_TILE = 512
+N_TILES = FEATURES // N_TILE
+EPS = 1e-8
+
+FLOPS = 2 * 2 * P * ROWS * FEATURES
+
+
+def tile_ca3_recurrentmatrix_pa_s_kernel(tc, current, memory_matrix, out):
+    nc = tc.nc
+    with ExitStack() as ctx:
+        keep = ctx.enter_context(tc.tile_pool(name="keep", bufs=1))
+        turn_psum = ctx.enter_context(tc.psum_pool(name="turn_psum", bufs=4))
+        mx_psum = ctx.enter_context(tc.psum_pool(name="mx_psum", bufs=2))
+        sim_psum = ctx.enter_context(tc.psum_pool(name="sim_psum", bufs=1))
+
+        cur_sb = keep.tile([P, FEATURES], BF16)
+        nc.sync.dma_start(out=cur_sb[:], in_=current)
+        mem_sb = keep.tile([P, PASSES, PACK, FEATURES], BF16)
+        mem_rows = memory_matrix.rearrange("(g p t) d -> p g t d", g=PASSES, t=PACK)
+        for k in range(CHUNKS):
+            g, t0 = divmod(CHUNK_TILES * k, PACK)
+            nc.sync.dma_start(
+                out=mem_sb[:, g, t0 : t0 + CHUNK_TILES, :],
+                in_=mem_rows[:, g, t0 : t0 + CHUNK_TILES, :],
+            )
+
+        ident_f32 = keep.tile([P, P], F32)
+        make_identity(nc, ident_f32[:])
+        ident_bf16 = keep.tile([P, P], BF16)
+        make_identity(nc, ident_bf16[:])
+
+        one = keep.tile([P, 1], F32)
+        nc.vector.memset(one[:], 1.0)
+        warm_sqrt = keep.tile([P, 1], F32)
+        nc.scalar.activation(out=warm_sqrt[:], in_=one[:], func=ACT.Sqrt)
+
+        cur_grouped = keep.tile([P, PASSES, P, PACK], BF16, align_bytes=64)
+        cur_codes = keep.tile([P, PASSES, P], U32, align_bytes=64)
+        cur_scales = keep.tile([P, PASSES, P], U8, align_bytes=64)
+        memT_grouped = keep.tile([P, ROW_TILES, PASSES, P, PACK], BF16, align_bytes=64)
+        memT_codes = keep.tile([P, ROW_TILES, PASSES, P], U32, align_bytes=64)
+        memT_scales = keep.tile([P, ROW_TILES, PASSES, P], U8, align_bytes=64)
+        mem_grouped = keep.tile([P, PASSES, FEATURES, PACK], BF16, align_bytes=64)
+        mem_codes = keep.tile([P, PASSES, FEATURES], U32, align_bytes=64)
+        mem_scales = keep.tile([P, PASSES, FEATURES], U8, align_bytes=64)
+        e_grouped = keep.tile([P, PASSES, P, PACK], BF16, align_bytes=64)
+        e_codes = keep.tile([P, PASSES, P], U32, align_bytes=64)
+        e_scales = keep.tile([P, PASSES, P], U8, align_bytes=64)
+
+        squares = keep.tile([P, ROW_TILES + 1, FEATURES], BF16)
+        mem_sumsq = keep.tile([P, ROW_TILES], F32)
+        mem_norm = keep.tile([P, ROW_TILES], F32)
+        mem_floor = keep.tile([P, ROW_TILES], F32)
+        mem_inv = keep.tile([P, ROW_TILES], F32)
+        cur_sumsq = keep.tile([P, 1], F32)
+        cur_norm = keep.tile([P, 1], F32)
+        cur_floor = keep.tile([P, 1], F32)
+        cur_inv = keep.tile([P, 1], F32)
+        simT_sb = keep.tile([P, ROW_TILES, P], F32)
+        sim_ps = [sim_psum.tile([P, N_TILE], F32, name="sim_ps%d" % g) for g in range(PASSES)]
+        chunk_max = keep.tile([P, CHUNKS], F32)
+
+        def turn_words(rows_bf16, grouped, copy):
+            words = rows_bf16.bitcast(F32)
+            turned = turn_psum.tile([P, WORD_BLOCKS, P], F32, tag="turn")
+            for w in range(WORD_BLOCKS):
+                nc.tensor.transpose(turned[:, w, :], words[:, w * P : (w + 1) * P], ident_f32[:])
+            copy(out=grouped.bitcast(F32), in_=turned[:].rearrange("p (q u) r -> p q r u", u=2))
+
+        def inverse_norm(sumsq, norm, floored, inverse):
+            nc.scalar.activation(out=norm, in_=sumsq, func=ACT.Sqrt)
+            nc.vector.tensor_scalar_max(out=floored, in0=norm, scalar1=EPS)
+            nc.vector.reciprocal(out=inverse, in_=floored)
+
+        turn_words(cur_sb[:], cur_grouped[:], nc.vector.tensor_copy)
+        nc.scalar.activation(
+            out=squares[:, ROW_TILES, :], in_=cur_sb[:], func=ACT.Square, accum_out=cur_sumsq[:]
+        )
+        inverse_norm(cur_sumsq[:], cur_norm[:], cur_floor[:], cur_inv[:])
+        nc.vector.quantize_mx(
+            out=cur_codes[:].rearrange("p q b -> p (q b)").bitcast(FP8X4),
+            scales=cur_scales[:].rearrange("p q b -> p (q b)"),
+            in_=cur_grouped[:].rearrange("p q b t -> p (q b t)"),
+        )
+        cur_fifth = keep.tile([P, FEATURES], F32)
+        nc.gpsimd.tensor_scalar(
+            out=cur_fifth[:], in0=cur_sb[:], scalar1=0.2, scalar2=0.0, op0=ALU.mult, op1=ALU.add
+        )
+
+        def turn_chunk(k):
+            for j in range(CHUNK_TILES * k, CHUNK_TILES * (k + 1)):
+                g, t = divmod(j, PACK)
+                copy = nc.vector.tensor_copy if j % 2 == 0 else nc.scalar.copy
+                turn_words(mem_sb[:, g, t, :], memT_grouped[:, j, :, :, :], copy)
+                nc.scalar.activation(
+                    out=squares[:, j, :],
+                    in_=mem_sb[:, g, t, :],
+                    func=ACT.Square,
+                    accum_out=mem_sumsq[:, j : j + 1],
+                )
+            tiles = slice(CHUNK_TILES * k, CHUNK_TILES * (k + 1))
+            inverse_norm(mem_sumsq[:, tiles], mem_norm[:, tiles], mem_floor[:, tiles], mem_inv[:, tiles])
+
+        def first_matmul_chunk(k):
+            tiles = slice(CHUNK_TILES * k, CHUNK_TILES * (k + 1))
+            nc.vector.quantize_mx(
+                out=memT_codes[:, tiles, :, :].rearrange("p j q c -> p (j q c)").bitcast(FP8X4),
+                scales=memT_scales[:, tiles, :, :].rearrange("p j q c -> p (j q c)"),
+                in_=memT_grouped[:, tiles, :, :, :].rearrange("p j q c t -> p (j q c t)"),
+            )
+            simT_ps = mx_psum.tile([P, CHUNK_TILES, P], F32, tag="mx")
+            for i in range(CHUNK_TILES):
+                j = CHUNK_TILES * k + i
+                for q in range(PASSES):
+                    nc.tensor.matmul_mx(
+                        out=simT_ps[:, i, :],
+                        lhsT=memT_codes[:, j, q, :].bitcast(FP8X4),
+                        lhsT_scale=memT_scales[:, j, q, :],
+                        rhs=cur_codes[:, q, :].bitcast(FP8X4),
+                        rhs_scale=cur_scales[:, q, :],
+                        start=(q == 0),
+                        stop=(q == PASSES - 1),
+                    )
+            for i in range(CHUNK_TILES):
+                j = CHUNK_TILES * k + i
+                nc.vector.tensor_scalar_mul(
+                    out=simT_sb[:, j, :], in0=simT_ps[:, i, :], scalar1=mem_inv[:, j : j + 1]
+                )
+
+        def turn_back_chunk(k):
+            g, t0 = divmod(CHUNK_TILES * k, PACK)
+            for t in range(t0, t0 + CHUNK_TILES):
+                nc.tensor.transpose(
+                    sim_ps[g][:, t * P : (t + 1) * P], simT_sb[:, PACK * g + t, :], ident_f32[:]
+                )
+            nc.vector.reduce_max(
+                out=chunk_max[:, k : k + 1],
+                in_=sim_ps[g][:, t0 * P : (t0 + CHUNK_TILES) * P],
+                axis=AXIS_X,
+            )
+
+        def second_operand(g):
+            for n in range(N_TILES):
+                cols = slice(n * N_TILE, (n + 1) * N_TILE)
+                nc.vector.tensor_copy(
+                    out=mem_grouped[:, g, cols, :].rearrange("p (c i) t -> p c t i", i=4),
+                    in_=mem_sb[:, g, :, cols].rearrange("p t (c i) -> p c t i", i=4),
+                )
+            for n in range(N_TILES):
+                cols = slice(n * N_TILE, (n + 1) * N_TILE)
+                nc.vector.quantize_mx(
+                    out=mem_codes[:, g, cols].bitcast(FP8X4),
+                    scales=mem_scales[:, g, cols],
+                    in_=mem_grouped[:, g, cols, :].rearrange("p d t -> p (d t)"),
+                )
+
+        for step in range(CHUNKS + 2):
+            if step < CHUNKS:
+                turn_chunk(step)
+            if 1 <= step <= CHUNKS:
+                first_matmul_chunk(step - 1)
+            if step >= 2:
+                turn_back_chunk(step - 2)
+            if step > 0 and step % HALF_CHUNKS == 0:
+                second_operand(step // HALF_CHUNKS - 1)
+
+        row_max = keep.tile([P, 1], F32)
+        nc.vector.reduce_max(out=row_max[:], in_=chunk_max[:], axis=AXIS_X)
+        exp_bias = keep.tile([P, 1], F32)
+        nc.vector.tensor_scalar(
+            out=exp_bias[:], in0=row_max[:], scalar1=cur_inv[:], scalar2=-1.0, op0=ALU.mult, op1=ALU.mult
+        )
+        e_sb = keep.tile([P, PASSES, N_TILE], BF16)
+        e_sum = keep.tile([P, PASSES], F32)
+        for g in range(PASSES):
+            nc.scalar.activation(
+                out=e_sb[:, g, :],
+                in_=sim_ps[g][:],
+                func=ACT.Exp,
+                bias=exp_bias[:],
+                scale=cur_inv[:],
+                accum_out=e_sum[:, g : g + 1],
+            )
+        for g in range(PASSES):
+            eT_ps = turn_psum.tile([P, PACK, P], BF16, tag="turn")
+            for t in range(PACK):
+                nc.tensor.transpose(eT_ps[:, t, :], e_sb[:, g, t * P : (t + 1) * P], ident_bf16[:])
+            nc.vector.tensor_copy(out=e_grouped[:, g, :, :], in_=eT_ps[:].rearrange("p t b -> p b t"))
+            nc.vector.quantize_mx(
+                out=e_codes[:, g, :].bitcast(FP8X4),
+                scales=e_scales[:, g, :],
+                in_=e_grouped[:, g, :, :].rearrange("p b t -> p (b t)"),
+            )
+
+        sum_scaled = keep.tile([P, 1], F32)
+        nc.vector.tensor_scalar(
+            out=sum_scaled[:], in0=e_sum[:, 0:1], scalar1=e_sum[:, 1:2], scalar2=1.25, op0=ALU.add, op1=ALU.mult
+        )
+        weight = keep.tile([P, 1], F32)
+        nc.vector.reciprocal(out=weight[:], in_=sum_scaled[:])
+
+        attracted = [mx_psum.tile([P, N_TILE], F32, tag="mx", name="attracted%d" % n) for n in range(N_TILES)]
+        for g in range(PASSES):
+            for n in range(N_TILES):
+                cols = slice(n * N_TILE, (n + 1) * N_TILE)
+                nc.tensor.matmul_mx(
+                    out=attracted[n][:],
+                    lhsT=e_codes[:, g, :].bitcast(FP8X4),
+                    lhsT_scale=e_scales[:, g, :],
+                    rhs=mem_codes[:, g, cols].bitcast(FP8X4),
+                    rhs_scale=mem_scales[:, g, cols],
+                    start=(g == 0),
+                    stop=(g == PASSES - 1),
+                )
+        out_sb = keep.tile([P, FEATURES], F32)
+        for n in range(N_TILES):
+            cols = slice(n * N_TILE, (n + 1) * N_TILE)
+            nc.vector.scalar_tensor_tensor(
+                out=out_sb[:, cols],
+                in0=attracted[n][:],
+                scalar=weight[:],
+                in1=cur_fifth[:, cols],
+                op0=ALU.mult,
+                op1=ALU.add,
+            )
+            nc.sync.dma_start(out=out[:, cols], in_=out_sb[:, cols])

@@ -21,7 +21,6 @@ PASSES = 2
 ROW_TILES = ROWS // P
 CHUNK_TILES = 2
 CHUNKS = ROW_TILES // CHUNK_TILES
-HALF_CHUNKS = CHUNKS // PASSES
 WORD_BLOCKS = FEATURES // 2 // P
 N_TILE = 512
 N_TILES = FEATURES // N_TILE
@@ -37,6 +36,7 @@ def tile_ca3_recurrentmatrix_pa_s_kernel(tc, current, memory_matrix, out):
         turn_psum = ctx.enter_context(tc.psum_pool(name="turn_psum", bufs=4))
         mx_psum = ctx.enter_context(tc.psum_pool(name="mx_psum", bufs=2))
         sim_psum = ctx.enter_context(tc.psum_pool(name="sim_psum", bufs=1))
+        ctx.enter_context(tc.manual_schedule())
 
         cur_sb = keep.tile([P, FEATURES], BF16)
         nc.sync.dma_start(out=cur_sb[:], in_=current)
@@ -53,11 +53,13 @@ def tile_ca3_recurrentmatrix_pa_s_kernel(tc, current, memory_matrix, out):
         make_identity(nc, ident_f32[:])
         ident_bf16 = keep.tile([P, P], BF16)
         make_identity(nc, ident_bf16[:])
+        minus_half = keep.tile([P, CHUNK_TILES], F32)
+        nc.gpsimd.memset(minus_half[:], -0.5)
 
-        one = keep.tile([P, 1], F32)
-        nc.vector.memset(one[:], 1.0)
-        warm_sqrt = keep.tile([P, 1], F32)
-        nc.scalar.activation(out=warm_sqrt[:], in_=one[:], func=ACT.Sqrt)
+        zero = keep.tile([P, 1], F32)
+        nc.vector.memset(zero[:], 0.0)
+        warm_exp = keep.tile([P, 1], F32)
+        nc.scalar.activation(out=warm_exp[:], in_=zero[:], func=ACT.Exp)
 
         cur_grouped = keep.tile([P, PASSES, P, PACK], BF16, align_bytes=64)
         cur_codes = keep.tile([P, PASSES, P], U32, align_bytes=64)
@@ -74,49 +76,66 @@ def tile_ca3_recurrentmatrix_pa_s_kernel(tc, current, memory_matrix, out):
 
         squares = keep.tile([P, ROW_TILES + 1, FEATURES], BF16)
         mem_sumsq = keep.tile([P, ROW_TILES], F32)
-        mem_norm = keep.tile([P, ROW_TILES], F32)
         mem_floor = keep.tile([P, ROW_TILES], F32)
         mem_inv = keep.tile([P, ROW_TILES], F32)
         cur_sumsq = keep.tile([P, 1], F32)
-        cur_norm = keep.tile([P, 1], F32)
         cur_floor = keep.tile([P, 1], F32)
         cur_inv = keep.tile([P, 1], F32)
         simT_sb = keep.tile([P, ROW_TILES, P], F32)
         sim_ps = [sim_psum.tile([P, N_TILE], F32, name="sim_ps%d" % g) for g in range(PASSES)]
         chunk_max = keep.tile([P, CHUNKS], F32)
+        turned = {}
+        simT_ps = {}
 
-        def turn_words(rows_bf16, grouped, copy):
+        def turn_words(rows_bf16):
             words = rows_bf16.bitcast(F32)
-            turned = turn_psum.tile([P, WORD_BLOCKS, P], F32, tag="turn")
+            bank = turn_psum.tile([P, WORD_BLOCKS, P], F32, tag="turn")
             for w in range(WORD_BLOCKS):
-                nc.tensor.transpose(turned[:, w, :], words[:, w * P : (w + 1) * P], ident_f32[:])
-            copy(out=grouped.bitcast(F32), in_=turned[:].rearrange("p (q u) r -> p q r u", u=2))
+                nc.tensor.transpose(bank[:, w, :], words[:, w * P : (w + 1) * P], ident_f32[:])
+            return bank
 
-        def inverse_norm(sumsq, norm, floored, inverse):
-            nc.scalar.activation(out=norm, in_=sumsq, func=ACT.Sqrt)
-            nc.vector.tensor_scalar_max(out=floored, in0=norm, scalar1=EPS)
-            nc.vector.reciprocal(out=inverse, in_=floored)
+        def group_words(bank, grouped):
+            nc.vector.tensor_copy(
+                out=grouped.bitcast(F32), in_=bank[:].rearrange("p (q u) r -> p q r u", u=2)
+            )
 
-        turn_words(cur_sb[:], cur_grouped[:], nc.vector.tensor_copy)
+        def inverse_norm(sumsq, floored, inverse):
+            nc.gpsimd.tensor_scalar_max(out=floored, in0=sumsq, scalar1=EPS * EPS)
+            nc.gpsimd.tensor_tensor(
+                out=inverse, in0=floored, in1=minus_half[:, 0 : sumsq.shape[1]], op=ALU.pow
+            )
+
+        def row_tiles(k):
+            return range(CHUNK_TILES * k, CHUNK_TILES * (k + 1))
+
+        cur_bank = turn_words(cur_sb[:])
+        group_words(cur_bank, cur_grouped[:])
         nc.scalar.activation(
             out=squares[:, ROW_TILES, :], in_=cur_sb[:], func=ACT.Square, accum_out=cur_sumsq[:]
-        )
-        inverse_norm(cur_sumsq[:], cur_norm[:], cur_floor[:], cur_inv[:])
-        nc.vector.quantize_mx(
-            out=cur_codes[:].rearrange("p q b -> p (q b)").bitcast(FP8X4),
-            scales=cur_scales[:].rearrange("p q b -> p (q b)"),
-            in_=cur_grouped[:].rearrange("p q b t -> p (q b t)"),
         )
         cur_fifth = keep.tile([P, FEATURES], F32)
         nc.gpsimd.tensor_scalar(
             out=cur_fifth[:], in0=cur_sb[:], scalar1=0.2, scalar2=0.0, op0=ALU.mult, op1=ALU.add
         )
+        inverse_norm(cur_sumsq[:], cur_floor[:], cur_inv[:])
+        nc.vector.quantize_mx(
+            out=cur_codes[:].rearrange("p q b -> p (q b)").bitcast(FP8X4),
+            scales=cur_scales[:].rearrange("p q b -> p (q b)"),
+            in_=cur_grouped[:].rearrange("p q b t -> p (q b t)"),
+        )
 
         def turn_chunk(k):
-            for j in range(CHUNK_TILES * k, CHUNK_TILES * (k + 1)):
+            for j in row_tiles(k):
                 g, t = divmod(j, PACK)
-                copy = nc.vector.tensor_copy if j % 2 == 0 else nc.scalar.copy
-                turn_words(mem_sb[:, g, t, :], memT_grouped[:, j, :, :, :], copy)
+                turned[j] = turn_words(mem_sb[:, g, t, :])
+
+        def group_chunk(k):
+            for j in row_tiles(k):
+                group_words(turned[j], memT_grouped[:, j, :, :, :])
+
+        def norms_chunk(k):
+            for j in row_tiles(k):
+                g, t = divmod(j, PACK)
                 nc.scalar.activation(
                     out=squares[:, j, :],
                     in_=mem_sb[:, g, t, :],
@@ -124,7 +143,7 @@ def tile_ca3_recurrentmatrix_pa_s_kernel(tc, current, memory_matrix, out):
                     accum_out=mem_sumsq[:, j : j + 1],
                 )
             tiles = slice(CHUNK_TILES * k, CHUNK_TILES * (k + 1))
-            inverse_norm(mem_sumsq[:, tiles], mem_norm[:, tiles], mem_floor[:, tiles], mem_inv[:, tiles])
+            inverse_norm(mem_sumsq[:, tiles], mem_floor[:, tiles], mem_inv[:, tiles])
 
         def first_matmul_chunk(k):
             tiles = slice(CHUNK_TILES * k, CHUNK_TILES * (k + 1))
@@ -133,12 +152,11 @@ def tile_ca3_recurrentmatrix_pa_s_kernel(tc, current, memory_matrix, out):
                 scales=memT_scales[:, tiles, :, :].rearrange("p j q c -> p (j q c)"),
                 in_=memT_grouped[:, tiles, :, :, :].rearrange("p j q c t -> p (j q c t)"),
             )
-            simT_ps = mx_psum.tile([P, CHUNK_TILES, P], F32, tag="mx")
-            for i in range(CHUNK_TILES):
-                j = CHUNK_TILES * k + i
+            simT_ps[k] = mx_psum.tile([P, CHUNK_TILES, P], F32, tag="mx", name="simT_ps%d" % k)
+            for i, j in enumerate(row_tiles(k)):
                 for q in range(PASSES):
                     nc.tensor.matmul_mx(
-                        out=simT_ps[:, i, :],
+                        out=simT_ps[k][:, i, :],
                         lhsT=memT_codes[:, j, q, :].bitcast(FP8X4),
                         lhsT_scale=memT_scales[:, j, q, :],
                         rhs=cur_codes[:, q, :].bitcast(FP8X4),
@@ -146,48 +164,58 @@ def tile_ca3_recurrentmatrix_pa_s_kernel(tc, current, memory_matrix, out):
                         start=(q == 0),
                         stop=(q == PASSES - 1),
                     )
-            for i in range(CHUNK_TILES):
-                j = CHUNK_TILES * k + i
-                nc.vector.tensor_scalar_mul(
-                    out=simT_sb[:, j, :], in0=simT_ps[:, i, :], scalar1=mem_inv[:, j : j + 1]
-                )
 
-        def turn_back_chunk(k):
-            g, t0 = divmod(CHUNK_TILES * k, PACK)
-            for t in range(t0, t0 + CHUNK_TILES):
-                nc.tensor.transpose(
-                    sim_ps[g][:, t * P : (t + 1) * P], simT_sb[:, PACK * g + t, :], ident_f32[:]
+        def scale_and_turn_back_chunk(k):
+            for i, j in enumerate(row_tiles(k)):
+                nc.vector.tensor_scalar_mul(
+                    out=simT_sb[:, j, :], in0=simT_ps[k][:, i, :], scalar1=mem_inv[:, j : j + 1]
                 )
+            for j in row_tiles(k):
+                g, t = divmod(j, PACK)
+                nc.tensor.transpose(sim_ps[g][:, t * P : (t + 1) * P], simT_sb[:, j, :], ident_f32[:])
+
+        def max_chunk(k):
+            g, t0 = divmod(CHUNK_TILES * k, PACK)
             nc.vector.reduce_max(
                 out=chunk_max[:, k : k + 1],
                 in_=sim_ps[g][:, t0 * P : (t0 + CHUNK_TILES) * P],
                 axis=AXIS_X,
             )
 
-        def second_operand(g):
-            for n in range(N_TILES):
-                cols = slice(n * N_TILE, (n + 1) * N_TILE)
-                nc.vector.tensor_copy(
-                    out=mem_grouped[:, g, cols, :].rearrange("p (c i) t -> p c t i", i=4),
-                    in_=mem_sb[:, g, :, cols].rearrange("p t (c i) -> p c t i", i=4),
-                )
-            for n in range(N_TILES):
-                cols = slice(n * N_TILE, (n + 1) * N_TILE)
-                nc.vector.quantize_mx(
-                    out=mem_codes[:, g, cols].bitcast(FP8X4),
-                    scales=mem_scales[:, g, cols],
-                    in_=mem_grouped[:, g, cols, :].rearrange("p d t -> p (d t)"),
-                )
+        def regroup(g, n, copy):
+            cols = slice(n * N_TILE, (n + 1) * N_TILE)
+            copy(
+                out=mem_grouped[:, g, cols, :].rearrange("p (c i) t -> p c t i", i=4),
+                in_=mem_sb[:, g, :, cols].rearrange("p t (c i) -> p c t i", i=4),
+            )
 
-        for step in range(CHUNKS + 2):
+        def quantise_regrouped(g, n):
+            cols = slice(n * N_TILE, (n + 1) * N_TILE)
+            nc.vector.quantize_mx(
+                out=mem_codes[:, g, cols].bitcast(FP8X4),
+                scales=mem_scales[:, g, cols],
+                in_=mem_grouped[:, g, cols, :].rearrange("p d t -> p (d t)"),
+            )
+
+        turn_chunk(0)
+        for step in range(CHUNKS + 3):
+            if step + 1 < CHUNKS:
+                turn_chunk(step + 1)
             if step < CHUNKS:
-                turn_chunk(step)
-            if 1 <= step <= CHUNKS:
+                group_chunk(step)
+                norms_chunk(step)
+            if 1 <= step < CHUNKS + 1:
                 first_matmul_chunk(step - 1)
-            if step >= 2:
-                turn_back_chunk(step - 2)
-            if step > 0 and step % HALF_CHUNKS == 0:
-                second_operand(step // HALF_CHUNKS - 1)
+            if 2 <= step < CHUNKS + 2:
+                scale_and_turn_back_chunk(step - 2)
+            if 3 <= step < 3 + N_TILES:
+                regroup(0, step - 3, nc.vector.tensor_copy)
+            if 3 + N_TILES <= step:
+                quantise_regrouped(0, step - 3 - N_TILES)
+            if 3 <= step:
+                max_chunk(step - 3)
+        for n in range(N_TILES):
+            regroup(1, n, nc.scalar.copy)
 
         row_max = keep.tile([P, 1], F32)
         nc.vector.reduce_max(out=row_max[:], in_=chunk_max[:], axis=AXIS_X)
@@ -197,6 +225,7 @@ def tile_ca3_recurrentmatrix_pa_s_kernel(tc, current, memory_matrix, out):
         )
         e_sb = keep.tile([P, PASSES, N_TILE], BF16)
         e_sum = keep.tile([P, PASSES], F32)
+        eT_ps = {}
         for g in range(PASSES):
             nc.scalar.activation(
                 out=e_sb[:, g, :],
@@ -206,11 +235,14 @@ def tile_ca3_recurrentmatrix_pa_s_kernel(tc, current, memory_matrix, out):
                 scale=cur_inv[:],
                 accum_out=e_sum[:, g : g + 1],
             )
-        for g in range(PASSES):
-            eT_ps = turn_psum.tile([P, PACK, P], BF16, tag="turn")
+            eT_ps[g] = turn_psum.tile([P, PACK, P], BF16, tag="turn", name="eT_ps%d" % g)
             for t in range(PACK):
-                nc.tensor.transpose(eT_ps[:, t, :], e_sb[:, g, t * P : (t + 1) * P], ident_bf16[:])
-            nc.vector.tensor_copy(out=e_grouped[:, g, :, :], in_=eT_ps[:].rearrange("p t b -> p b t"))
+                nc.tensor.transpose(eT_ps[g][:, t, :], e_sb[:, g, t * P : (t + 1) * P], ident_bf16[:])
+        for n in range(N_TILES):
+            quantise_regrouped(1, n)
+        for g in range(PASSES):
+            copy = nc.vector.tensor_copy if g == 0 else nc.scalar.copy
+            copy(out=e_grouped[:, g, :, :], in_=eT_ps[g][:].rearrange("p t b -> p b t"))
             nc.vector.quantize_mx(
                 out=e_codes[:, g, :].bitcast(FP8X4),
                 scales=e_scales[:, g, :],

@@ -25,6 +25,7 @@ WORD_BLOCKS = FEATURES // 2 // P
 N_TILE = 512
 N_TILES = FEATURES // N_TILE
 EPS = 1e-8
+SCALAR_COLS = 1024
 
 FLOPS = 2 * 2 * P * ROWS * FEATURES
 
@@ -166,10 +167,13 @@ def tile_ca3_recurrentmatrix_pa_s_kernel(tc, current, memory_matrix, out):
                     )
 
         def scale_and_turn_back_chunk(k):
-            for i, j in enumerate(row_tiles(k)):
-                nc.vector.tensor_scalar_mul(
-                    out=simT_sb[:, j, :], in0=simT_ps[k][:, i, :], scalar1=mem_inv[:, j : j + 1]
-                )
+            tiles = slice(CHUNK_TILES * k, CHUNK_TILES * (k + 1))
+            nc.vector.tensor_tensor(
+                out=simT_sb[:, tiles, :],
+                in0=simT_ps[k][:],
+                in1=mem_inv[:, tiles].unsqueeze(2).to_broadcast([P, CHUNK_TILES, P]),
+                op=ALU.mult,
+            )
             for j in row_tiles(k):
                 g, t = divmod(j, PACK)
                 nc.tensor.transpose(sim_ps[g][:, t * P : (t + 1) * P], simT_sb[:, j, :], ident_f32[:])
@@ -182,8 +186,8 @@ def tile_ca3_recurrentmatrix_pa_s_kernel(tc, current, memory_matrix, out):
                 axis=AXIS_X,
             )
 
-        def regroup(g, n, copy):
-            cols = slice(n * N_TILE, (n + 1) * N_TILE)
+        def regroup(g, first, last, copy):
+            cols = slice(first, last)
             copy(
                 out=mem_grouped[:, g, cols, :].rearrange("p (c i) t -> p c t i", i=4),
                 in_=mem_sb[:, g, :, cols].rearrange("p t (c i) -> p c t i", i=4),
@@ -209,13 +213,11 @@ def tile_ca3_recurrentmatrix_pa_s_kernel(tc, current, memory_matrix, out):
             if 2 <= step < CHUNKS + 2:
                 scale_and_turn_back_chunk(step - 2)
             if 3 <= step < 3 + N_TILES:
-                regroup(0, step - 3, nc.vector.tensor_copy)
-            if 3 + N_TILES <= step:
-                quantise_regrouped(0, step - 3 - N_TILES)
+                regroup(0, (step - 3) * N_TILE, (step - 2) * N_TILE, nc.vector.tensor_copy)
             if 3 <= step:
                 max_chunk(step - 3)
-        for n in range(N_TILES):
-            regroup(1, n, nc.scalar.copy)
+        regroup(1, 0, N_TILE, nc.scalar.copy)
+        regroup(1, N_TILE, SCALAR_COLS, nc.scalar.copy)
 
         row_max = keep.tile([P, 1], F32)
         nc.vector.reduce_max(out=row_max[:], in_=chunk_max[:], axis=AXIS_X)
@@ -238,11 +240,11 @@ def tile_ca3_recurrentmatrix_pa_s_kernel(tc, current, memory_matrix, out):
             eT_ps[g] = turn_psum.tile([P, PACK, P], BF16, tag="turn", name="eT_ps%d" % g)
             for t in range(PACK):
                 nc.tensor.transpose(eT_ps[g][:, t, :], e_sb[:, g, t * P : (t + 1) * P], ident_bf16[:])
-        for n in range(N_TILES):
-            quantise_regrouped(1, n)
         for g in range(PASSES):
-            copy = nc.vector.tensor_copy if g == 0 else nc.scalar.copy
-            copy(out=e_grouped[:, g, :, :], in_=eT_ps[g][:].rearrange("p t b -> p b t"))
+            for n in range(N_TILES):
+                quantise_regrouped(g, n)
+        for g in range(PASSES):
+            nc.scalar.copy(out=e_grouped[:, g, :, :], in_=eT_ps[g][:].rearrange("p t b -> p b t"))
             nc.vector.quantize_mx(
                 out=e_codes[:, g, :].bitcast(FP8X4),
                 scales=e_scales[:, g, :],

@@ -24,8 +24,9 @@ CHUNKS = ROW_TILES // CHUNK_TILES
 WORD_BLOCKS = FEATURES // 2 // P
 N_TILE = 512
 N_TILES = FEATURES // N_TILE
+OUT_TILE = 256
 EPS = 1e-8
-SCALAR_COLS = 1024
+LOADS = ((0, 1), (1, 2), (2, 4), (4, 6), (6, 8))
 
 FLOPS = 2 * 2 * P * ROWS * FEATURES
 
@@ -43,17 +44,15 @@ def tile_ca3_recurrentmatrix_pa_s_kernel(tc, current, memory_matrix, out):
         nc.sync.dma_start(out=cur_sb[:], in_=current)
         mem_sb = keep.tile([P, PASSES, PACK, FEATURES], BF16)
         mem_rows = memory_matrix.rearrange("(g p t) d -> p g t d", g=PASSES, t=PACK)
-        for k in range(CHUNKS):
-            g, t0 = divmod(CHUNK_TILES * k, PACK)
+        for first, last in LOADS:
+            g, t0 = divmod(first, PACK)
             nc.sync.dma_start(
-                out=mem_sb[:, g, t0 : t0 + CHUNK_TILES, :],
-                in_=mem_rows[:, g, t0 : t0 + CHUNK_TILES, :],
+                out=mem_sb[:, g, t0 : t0 + last - first, :],
+                in_=mem_rows[:, g, t0 : t0 + last - first, :],
             )
 
         ident_f32 = keep.tile([P, P], F32)
         make_identity(nc, ident_f32[:])
-        ident_bf16 = keep.tile([P, P], BF16)
-        make_identity(nc, ident_bf16[:])
         minus_half = keep.tile([P, CHUNK_TILES], F32)
         nc.gpsimd.memset(minus_half[:], -0.5)
 
@@ -75,7 +74,8 @@ def tile_ca3_recurrentmatrix_pa_s_kernel(tc, current, memory_matrix, out):
         e_codes = keep.tile([P, PASSES, P], U32, align_bytes=64)
         e_scales = keep.tile([P, PASSES, P], U8, align_bytes=64)
 
-        squares = keep.tile([P, ROW_TILES + 1, FEATURES], BF16)
+        scalar_squares = keep.tile([P, FEATURES], BF16)
+        cur_squares = keep.tile([P, FEATURES], F32)
         mem_sumsq = keep.tile([P, ROW_TILES], F32)
         mem_floor = keep.tile([P, ROW_TILES], F32)
         mem_inv = keep.tile([P, ROW_TILES], F32)
@@ -84,9 +84,8 @@ def tile_ca3_recurrentmatrix_pa_s_kernel(tc, current, memory_matrix, out):
         cur_inv = keep.tile([P, 1], F32)
         simT_sb = keep.tile([P, ROW_TILES, P], F32)
         sim_ps = [sim_psum.tile([P, N_TILE], F32, name="sim_ps%d" % g) for g in range(PASSES)]
-        chunk_max = keep.tile([P, CHUNKS], F32)
+        half_max = keep.tile([P, PASSES], F32)
         turned = {}
-        simT_ps = {}
 
         def turn_words(rows_bf16):
             words = rows_bf16.bitcast(F32)
@@ -95,10 +94,8 @@ def tile_ca3_recurrentmatrix_pa_s_kernel(tc, current, memory_matrix, out):
                 nc.tensor.transpose(bank[:, w, :], words[:, w * P : (w + 1) * P], ident_f32[:])
             return bank
 
-        def group_words(bank, grouped):
-            nc.vector.tensor_copy(
-                out=grouped.bitcast(F32), in_=bank[:].rearrange("p (q u) r -> p q r u", u=2)
-            )
+        def group_words(bank, grouped, copy):
+            copy(out=grouped.bitcast(F32), in_=bank[:].rearrange("p (q u) r -> p q r u", u=2))
 
         def inverse_norm(sumsq, floored, inverse):
             nc.gpsimd.tensor_scalar_max(out=floored, in0=sumsq, scalar1=EPS * EPS)
@@ -109,55 +106,37 @@ def tile_ca3_recurrentmatrix_pa_s_kernel(tc, current, memory_matrix, out):
         def row_tiles(k):
             return range(CHUNK_TILES * k, CHUNK_TILES * (k + 1))
 
-        cur_bank = turn_words(cur_sb[:])
-        group_words(cur_bank, cur_grouped[:])
-        nc.scalar.activation(
-            out=squares[:, ROW_TILES, :], in_=cur_sb[:], func=ACT.Square, accum_out=cur_sumsq[:]
-        )
-        cur_fifth = keep.tile([P, FEATURES], F32)
-        nc.gpsimd.tensor_scalar(
-            out=cur_fifth[:], in0=cur_sb[:], scalar1=0.2, scalar2=0.0, op0=ALU.mult, op1=ALU.add
-        )
-        inverse_norm(cur_sumsq[:], cur_floor[:], cur_inv[:])
-        nc.vector.quantize_mx(
-            out=cur_codes[:].rearrange("p q b -> p (q b)").bitcast(FP8X4),
-            scales=cur_scales[:].rearrange("p q b -> p (q b)"),
-            in_=cur_grouped[:].rearrange("p q b t -> p (q b t)"),
-        )
+        def turn_tile(j):
+            g, t = divmod(j, PACK)
+            turned[j] = turn_words(mem_sb[:, g, t, :])
 
-        def turn_chunk(k):
-            for j in row_tiles(k):
-                g, t = divmod(j, PACK)
-                turned[j] = turn_words(mem_sb[:, g, t, :])
+        def group_tile(j, copy):
+            group_words(turned[j], memT_grouped[:, j, :, :, :], copy)
 
-        def group_chunk(k):
-            for j in row_tiles(k):
-                group_words(turned[j], memT_grouped[:, j, :, :, :])
+        def norm_tile(j):
+            g, t = divmod(j, PACK)
+            nc.scalar.activation(
+                out=scalar_squares[:], in_=mem_sb[:, g, t, :], func=ACT.Square, accum_out=mem_sumsq[:, j : j + 1]
+            )
 
-        def norms_chunk(k):
-            for j in row_tiles(k):
-                g, t = divmod(j, PACK)
-                nc.scalar.activation(
-                    out=squares[:, j, :],
-                    in_=mem_sb[:, g, t, :],
-                    func=ACT.Square,
-                    accum_out=mem_sumsq[:, j : j + 1],
-                )
-            tiles = slice(CHUNK_TILES * k, CHUNK_TILES * (k + 1))
+        def inverse_norms(first, last):
+            tiles = slice(first, last)
             inverse_norm(mem_sumsq[:, tiles], mem_floor[:, tiles], mem_inv[:, tiles])
 
-        def first_matmul_chunk(k):
+        def quantise_chunk(k):
             tiles = slice(CHUNK_TILES * k, CHUNK_TILES * (k + 1))
             nc.vector.quantize_mx(
                 out=memT_codes[:, tiles, :, :].rearrange("p j q c -> p (j q c)").bitcast(FP8X4),
                 scales=memT_scales[:, tiles, :, :].rearrange("p j q c -> p (j q c)"),
                 in_=memT_grouped[:, tiles, :, :, :].rearrange("p j q c t -> p (j q c t)"),
             )
-            simT_ps[k] = mx_psum.tile([P, CHUNK_TILES, P], F32, tag="mx", name="simT_ps%d" % k)
-            for i, j in enumerate(row_tiles(k)):
+
+        def first_matmul_chunk(k):
+            for j in row_tiles(k):
+                g, t = divmod(j, PACK)
                 for q in range(PASSES):
                     nc.tensor.matmul_mx(
-                        out=simT_ps[k][:, i, :],
+                        out=simT_ps[g][:, t, :],
                         lhsT=memT_codes[:, j, q, :].bitcast(FP8X4),
                         lhsT_scale=memT_scales[:, j, q, :],
                         rhs=cur_codes[:, q, :].bitcast(FP8X4),
@@ -166,25 +145,21 @@ def tile_ca3_recurrentmatrix_pa_s_kernel(tc, current, memory_matrix, out):
                         stop=(q == PASSES - 1),
                     )
 
-        def scale_and_turn_back_chunk(k):
-            tiles = slice(CHUNK_TILES * k, CHUNK_TILES * (k + 1))
+        def scale_half(g):
+            tiles = slice(PACK * g, PACK * (g + 1))
             nc.vector.tensor_tensor(
                 out=simT_sb[:, tiles, :],
-                in0=simT_ps[k][:],
-                in1=mem_inv[:, tiles].unsqueeze(2).to_broadcast([P, CHUNK_TILES, P]),
+                in0=simT_ps[g][:],
+                in1=mem_inv[:, tiles].unsqueeze(2).to_broadcast([P, PACK, P]),
                 op=ALU.mult,
             )
-            for j in row_tiles(k):
-                g, t = divmod(j, PACK)
-                nc.tensor.transpose(sim_ps[g][:, t * P : (t + 1) * P], simT_sb[:, j, :], ident_f32[:])
 
-        def max_chunk(k):
-            g, t0 = divmod(CHUNK_TILES * k, PACK)
-            nc.vector.reduce_max(
-                out=chunk_max[:, k : k + 1],
-                in_=sim_ps[g][:, t0 * P : (t0 + CHUNK_TILES) * P],
-                axis=AXIS_X,
-            )
+        def turn_back_half(g):
+            for t in range(PACK):
+                nc.tensor.transpose(sim_ps[g][:, t * P : (t + 1) * P], simT_sb[:, PACK * g + t, :], ident_f32[:])
+
+        def max_half(g):
+            nc.vector.reduce_max(out=half_max[:, g : g + 1], in_=sim_ps[g][:], axis=AXIS_X)
 
         def regroup(g, first, last, copy):
             cols = slice(first, last)
@@ -201,26 +176,64 @@ def tile_ca3_recurrentmatrix_pa_s_kernel(tc, current, memory_matrix, out):
                 in_=mem_grouped[:, g, cols, :].rearrange("p d t -> p (d t)"),
             )
 
-        turn_chunk(0)
-        for step in range(CHUNKS + 3):
-            if step + 1 < CHUNKS:
-                turn_chunk(step + 1)
-            if step < CHUNKS:
-                group_chunk(step)
-                norms_chunk(step)
-            if 1 <= step < CHUNKS + 1:
-                first_matmul_chunk(step - 1)
-            if 2 <= step < CHUNKS + 2:
-                scale_and_turn_back_chunk(step - 2)
-            if 3 <= step < 3 + N_TILES:
-                regroup(0, (step - 3) * N_TILE, (step - 2) * N_TILE, nc.vector.tensor_copy)
-            if 3 <= step:
-                max_chunk(step - 3)
+        cur_bank = turn_words(cur_sb[:])
+        nc.vector.scalar_tensor_tensor(
+            out=cur_squares[:],
+            in0=cur_sb[:],
+            scalar=1.0,
+            in1=cur_sb[:],
+            op0=ALU.mult,
+            op1=ALU.mult,
+            accum_out=cur_sumsq[:],
+        )
+        group_words(cur_bank, cur_grouped[:], nc.vector.tensor_copy)
+        turn_tile(0)
+        norm_tile(0)
+        group_tile(0, nc.vector.tensor_copy)
+        nc.vector.quantize_mx(
+            out=cur_codes[:].rearrange("p q b -> p (q b)").bitcast(FP8X4),
+            scales=cur_scales[:].rearrange("p q b -> p (q b)"),
+            in_=cur_grouped[:].rearrange("p q b t -> p (q b t)"),
+        )
+        turn_tile(1)
+        norm_tile(1)
+        group_tile(1, nc.vector.tensor_copy)
+        inverse_norms(0, 2)
+        quantise_chunk(0)
+        turn_tile(2)
+        turn_tile(3)
+        inverse_norm(cur_sumsq[:], cur_floor[:], cur_inv[:])
+        simT_ps = [mx_psum.tile([P, PACK, P], F32, tag="mx", name="simT_ps%d" % g) for g in range(PASSES)]
+        for k in range(1, CHUNKS):
+            for j in row_tiles(k):
+                group_tile(j, nc.vector.tensor_copy)
+                norm_tile(j)
+                if k == CHUNKS - 1:
+                    inverse_norms(j, j + 1)
+            if k < CHUNKS - 1:
+                inverse_norms(CHUNK_TILES * k, CHUNK_TILES * (k + 1))
+            quantise_chunk(k)
+            if k + 1 < CHUNKS:
+                for j in row_tiles(k + 1):
+                    turn_tile(j)
+            first_matmul_chunk(k - 1)
+        first_matmul_chunk(CHUNKS - 1)
+        scale_half(0)
+        turn_back_half(0)
+        regroup(0, 0, N_TILE // 2, nc.vector.tensor_copy)
+        scale_half(1)
+        turn_back_half(1)
+        for g in range(PASSES):
+            max_half(g)
         regroup(1, 0, N_TILE, nc.scalar.copy)
-        regroup(1, N_TILE, SCALAR_COLS, nc.scalar.copy)
+        regroup(1, N_TILE, FEATURES, nc.scalar.copy)
+        cur_fifth = keep.tile([P, FEATURES], F32)
+        nc.gpsimd.tensor_scalar(
+            out=cur_fifth[:], in0=cur_sb[:], scalar1=0.2, scalar2=0.0, op0=ALU.mult, op1=ALU.add
+        )
 
         row_max = keep.tile([P, 1], F32)
-        nc.vector.reduce_max(out=row_max[:], in_=chunk_max[:], axis=AXIS_X)
+        nc.vector.reduce_max(out=row_max[:], in_=half_max[:], axis=AXIS_X)
         exp_bias = keep.tile([P, 1], F32)
         nc.vector.tensor_scalar(
             out=exp_bias[:], in0=row_max[:], scalar1=cur_inv[:], scalar2=-1.0, op0=ALU.mult, op1=ALU.mult
@@ -230,26 +243,35 @@ def tile_ca3_recurrentmatrix_pa_s_kernel(tc, current, memory_matrix, out):
         eT_ps = {}
         for g in range(PASSES):
             nc.scalar.activation(
-                out=e_sb[:, g, :],
-                in_=sim_ps[g][:],
+                out=e_sb[:, g, :].rearrange("b (u p i) -> b u p i", u=2, i=2),
+                in_=sim_ps[g][:].rearrange("b (u i p) -> b u p i", u=2, i=2),
                 func=ACT.Exp,
                 bias=exp_bias[:],
                 scale=cur_inv[:],
                 accum_out=e_sum[:, g : g + 1],
             )
-            eT_ps[g] = turn_psum.tile([P, PACK, P], BF16, tag="turn", name="eT_ps%d" % g)
-            for t in range(PACK):
-                nc.tensor.transpose(eT_ps[g][:, t, :], e_sb[:, g, t * P : (t + 1) * P], ident_bf16[:])
+            eT_ps[g] = turn_psum.tile([P, 2, P], F32, tag="turn", name="eT_ps%d" % g)
+            words = e_sb[:, g, :].bitcast(F32)
+            for u in range(2):
+                nc.tensor.transpose(eT_ps[g][:, u, :], words[:, u * P : (u + 1) * P], ident_f32[:])
         for g in range(PASSES):
-            for n in range(N_TILES):
-                quantise_regrouped(g, n)
-        for g in range(PASSES):
-            nc.scalar.copy(out=e_grouped[:, g, :, :], in_=eT_ps[g][:].rearrange("p t b -> p b t"))
+            nc.scalar.copy(out=e_grouped[:, g, :, :].bitcast(F32), in_=eT_ps[g][:].rearrange("p u b -> p b u"))
+        regroup(0, FEATURES - N_TILE // 2, FEATURES, nc.scalar.copy)
+        regroup(0, N_TILE // 2, N_TILE, nc.vector.tensor_copy)
+        regroup(0, N_TILE, FEATURES - N_TILE // 2, nc.vector.tensor_copy)
+
+        def quantise_e(g):
             nc.vector.quantize_mx(
                 out=e_codes[:, g, :].bitcast(FP8X4),
                 scales=e_scales[:, g, :],
                 in_=e_grouped[:, g, :, :].rearrange("p b t -> p (b t)"),
             )
+
+        quantise_regrouped(0, 0)
+        quantise_regrouped(1, 0)
+        quantise_e(0)
+        quantise_regrouped(1, 1)
+        quantise_e(1)
 
         sum_scaled = keep.tile([P, 1], F32)
         nc.vector.tensor_scalar(
@@ -258,25 +280,26 @@ def tile_ca3_recurrentmatrix_pa_s_kernel(tc, current, memory_matrix, out):
         weight = keep.tile([P, 1], F32)
         nc.vector.reciprocal(out=weight[:], in_=sum_scaled[:])
 
+        quantise_regrouped(0, 1)
         attracted = [mx_psum.tile([P, N_TILE], F32, tag="mx", name="attracted%d" % n) for n in range(N_TILES)]
-        for g in range(PASSES):
-            for n in range(N_TILES):
-                cols = slice(n * N_TILE, (n + 1) * N_TILE)
-                nc.tensor.matmul_mx(
-                    out=attracted[n][:],
-                    lhsT=e_codes[:, g, :].bitcast(FP8X4),
-                    lhsT_scale=e_scales[:, g, :],
-                    rhs=mem_codes[:, g, cols].bitcast(FP8X4),
-                    rhs_scale=mem_scales[:, g, cols],
-                    start=(g == 0),
-                    stop=(g == PASSES - 1),
-                )
-        out_sb = keep.tile([P, FEATURES], F32)
-        for n in range(N_TILES):
+        for n, g, start, stop in ((0, 0, True, False), (0, 1, False, True), (1, 1, True, False), (1, 0, False, True)):
             cols = slice(n * N_TILE, (n + 1) * N_TILE)
+            nc.tensor.matmul_mx(
+                out=attracted[n][:],
+                lhsT=e_codes[:, g, :].bitcast(FP8X4),
+                lhsT_scale=e_scales[:, g, :],
+                rhs=mem_codes[:, g, cols].bitcast(FP8X4),
+                rhs_scale=mem_scales[:, g, cols],
+                start=start,
+                stop=stop,
+            )
+        out_sb = keep.tile([P, FEATURES], F32)
+        for first in range(0, FEATURES, OUT_TILE):
+            cols = slice(first, first + OUT_TILE)
+            n, offset = divmod(first, N_TILE)
             nc.vector.scalar_tensor_tensor(
                 out=out_sb[:, cols],
-                in0=attracted[n][:],
+                in0=attracted[n][:, offset : offset + OUT_TILE],
                 scalar=weight[:],
                 in1=cur_fifth[:, cols],
                 op0=ALU.mult,

@@ -176,6 +176,11 @@ def tile_ca3_recurrentmatrix_pa_s_kernel(tc, current, memory_matrix, out):
                 in_=mem_grouped[:, g, cols, :].rearrange("p d t -> p (d t)"),
             )
 
+        def keep_warm(bank, count):
+            for i in range(count):
+                nc.tensor.matmul(bank[:, 0:P], lhsT=ident_f32[:], rhs=ident_f32[:], start=True, stop=True)
+
+        keep_warm(sim_ps[1], 4)
         cur_bank = turn_words(cur_sb[:])
         nc.vector.scalar_tensor_tensor(
             out=cur_squares[:],
@@ -202,6 +207,7 @@ def tile_ca3_recurrentmatrix_pa_s_kernel(tc, current, memory_matrix, out):
         quantise_chunk(0)
         turn_tile(2)
         turn_tile(3)
+        keep_warm(sim_ps[1], 1)
         inverse_norm(cur_sumsq[:], cur_floor[:], cur_inv[:])
         simT_ps = [mx_psum.tile([P, PACK, P], F32, tag="mx", name="simT_ps%d" % g) for g in range(PASSES)]
         for k in range(1, CHUNKS):
@@ -216,6 +222,7 @@ def tile_ca3_recurrentmatrix_pa_s_kernel(tc, current, memory_matrix, out):
             if k + 1 < CHUNKS:
                 for j in row_tiles(k + 1):
                     turn_tile(j)
+                keep_warm(sim_ps[1], 1)
             first_matmul_chunk(k - 1)
         first_matmul_chunk(CHUNKS - 1)
         scale_half(0)
@@ -231,6 +238,9 @@ def tile_ca3_recurrentmatrix_pa_s_kernel(tc, current, memory_matrix, out):
         nc.gpsimd.tensor_scalar(
             out=cur_fifth[:], in0=cur_sb[:], scalar1=0.2, scalar2=0.0, op0=ALU.mult, op1=ALU.add
         )
+
+        idle_ps = turn_psum.tile([P, N_TILE], F32, tag="turn", name="idle_ps")
+        keep_warm(idle_ps, 3)
 
         row_max = keep.tile([P, 1], F32)
         nc.vector.reduce_max(out=row_max[:], in_=half_max[:], axis=AXIS_X)
@@ -280,6 +290,7 @@ def tile_ca3_recurrentmatrix_pa_s_kernel(tc, current, memory_matrix, out):
         weight = keep.tile([P, 1], F32)
         nc.vector.reciprocal(out=weight[:], in_=sum_scaled[:])
 
+        keep_warm(idle_ps, 2)
         quantise_regrouped(0, 1)
         attracted = [mx_psum.tile([P, N_TILE], F32, tag="mx", name="attracted%d" % n) for n in range(N_TILES)]
         for n, g, start, stop in ((0, 0, True, False), (0, 1, False, True), (1, 1, True, False), (1, 0, False, True)):

@@ -180,7 +180,7 @@ def tile_ca3_recurrentmatrix_pa_s_kernel(tc, current, memory_matrix, out):
             for i in range(count):
                 nc.tensor.matmul(bank[:, 0:P], lhsT=ident_f32[:], rhs=ident_f32[:], start=True, stop=True)
 
-        keep_warm(sim_ps[1], 4)
+        keep_warm(sim_ps[1], 2)
         cur_bank = turn_words(cur_sb[:])
         nc.vector.scalar_tensor_tensor(
             out=cur_squares[:],
@@ -192,6 +192,11 @@ def tile_ca3_recurrentmatrix_pa_s_kernel(tc, current, memory_matrix, out):
             accum_out=cur_sumsq[:],
         )
         group_words(cur_bank, cur_grouped[:], nc.vector.tensor_copy)
+        inverse_norm(cur_sumsq[:], cur_floor[:], cur_inv[:])
+        cur_fifth = keep.tile([P, FEATURES], F32)
+        nc.gpsimd.tensor_scalar(
+            out=cur_fifth[:], in0=cur_sb[:], scalar1=0.2, scalar2=0.0, op0=ALU.mult, op1=ALU.add
+        )
         turn_tile(0)
         norm_tile(0)
         group_tile(0, nc.vector.tensor_copy)
@@ -208,7 +213,6 @@ def tile_ca3_recurrentmatrix_pa_s_kernel(tc, current, memory_matrix, out):
         turn_tile(2)
         turn_tile(3)
         keep_warm(sim_ps[1], 1)
-        inverse_norm(cur_sumsq[:], cur_floor[:], cur_inv[:])
         simT_ps = [mx_psum.tile([P, PACK, P], F32, tag="mx", name="simT_ps%d" % g) for g in range(PASSES)]
         for k in range(1, CHUNKS):
             for j in row_tiles(k):
@@ -234,10 +238,6 @@ def tile_ca3_recurrentmatrix_pa_s_kernel(tc, current, memory_matrix, out):
             max_half(g)
         regroup(1, 0, N_TILE, nc.scalar.copy)
         regroup(1, N_TILE, FEATURES, nc.scalar.copy)
-        cur_fifth = keep.tile([P, FEATURES], F32)
-        nc.gpsimd.tensor_scalar(
-            out=cur_fifth[:], in0=cur_sb[:], scalar1=0.2, scalar2=0.0, op0=ALU.mult, op1=ALU.add
-        )
 
         idle_ps = turn_psum.tile([P, N_TILE], F32, tag="turn", name="idle_ps")
         keep_warm(idle_ps, 3)

@@ -53,7 +53,7 @@ def tile_ca3_recurrentmatrix_pa_s_kernel(tc, current, memory_matrix, out):
 
         ident_f32 = keep.tile([P, P], F32)
         make_identity(nc, ident_f32[:])
-        minus_half = keep.tile([P, CHUNK_TILES], F32)
+        minus_half = keep.tile([P, PACK], F32)
         nc.gpsimd.memset(minus_half[:], -0.5)
 
         zero = keep.tile([P, 1], F32)
@@ -74,6 +74,7 @@ def tile_ca3_recurrentmatrix_pa_s_kernel(tc, current, memory_matrix, out):
         e_codes = keep.tile([P, PASSES, P], U32, align_bytes=64)
         e_scales = keep.tile([P, PASSES, P], U8, align_bytes=64)
 
+        cur_fifth = keep.tile([P, FEATURES], F32)
         scalar_squares = keep.tile([P, FEATURES], BF16)
         cur_squares = keep.tile([P, FEATURES], F32)
         mem_sumsq = keep.tile([P, ROW_TILES], F32)
@@ -97,10 +98,12 @@ def tile_ca3_recurrentmatrix_pa_s_kernel(tc, current, memory_matrix, out):
         def group_words(bank, grouped, copy):
             copy(out=grouped.bitcast(F32), in_=bank[:].rearrange("p (q u) r -> p q r u", u=2))
 
-        def inverse_norm(sumsq, floored, inverse):
+        def floor_squares(sumsq, floored):
             nc.gpsimd.tensor_scalar_max(out=floored, in0=sumsq, scalar1=EPS * EPS)
+
+        def invert(floored, inverse):
             nc.gpsimd.tensor_tensor(
-                out=inverse, in0=floored, in1=minus_half[:, 0 : sumsq.shape[1]], op=ALU.pow
+                out=inverse, in0=floored, in1=minus_half[:, 0 : floored.shape[1]], op=ALU.pow
             )
 
         def row_tiles(k):
@@ -119,9 +122,11 @@ def tile_ca3_recurrentmatrix_pa_s_kernel(tc, current, memory_matrix, out):
                 out=scalar_squares[:], in_=mem_sb[:, g, t, :], func=ACT.Square, accum_out=mem_sumsq[:, j : j + 1]
             )
 
-        def inverse_norms(first, last):
-            tiles = slice(first, last)
-            inverse_norm(mem_sumsq[:, tiles], mem_floor[:, tiles], mem_inv[:, tiles])
+        def floor_tiles(first, last):
+            floor_squares(mem_sumsq[:, first:last], mem_floor[:, first:last])
+
+        def invert_tiles(first, last):
+            invert(mem_floor[:, first:last], mem_inv[:, first:last])
 
         def quantise_chunk(k):
             tiles = slice(CHUNK_TILES * k, CHUNK_TILES * (k + 1))
@@ -192,11 +197,8 @@ def tile_ca3_recurrentmatrix_pa_s_kernel(tc, current, memory_matrix, out):
             accum_out=cur_sumsq[:],
         )
         group_words(cur_bank, cur_grouped[:], nc.vector.tensor_copy)
-        inverse_norm(cur_sumsq[:], cur_floor[:], cur_inv[:])
-        cur_fifth = keep.tile([P, FEATURES], F32)
-        nc.gpsimd.tensor_scalar(
-            out=cur_fifth[:], in0=cur_sb[:], scalar1=0.2, scalar2=0.0, op0=ALU.mult, op1=ALU.add
-        )
+        floor_squares(cur_sumsq[:], cur_floor[:])
+        invert(cur_floor[:], cur_inv[:])
         turn_tile(0)
         norm_tile(0)
         group_tile(0, nc.vector.tensor_copy)
@@ -208,7 +210,6 @@ def tile_ca3_recurrentmatrix_pa_s_kernel(tc, current, memory_matrix, out):
         turn_tile(1)
         norm_tile(1)
         group_tile(1, nc.vector.tensor_copy)
-        inverse_norms(0, 2)
         quantise_chunk(0)
         turn_tile(2)
         turn_tile(3)
@@ -218,10 +219,17 @@ def tile_ca3_recurrentmatrix_pa_s_kernel(tc, current, memory_matrix, out):
             for j in row_tiles(k):
                 group_tile(j, nc.vector.tensor_copy)
                 norm_tile(j)
-                if k == CHUNKS - 1:
-                    inverse_norms(j, j + 1)
-            if k < CHUNKS - 1:
-                inverse_norms(CHUNK_TILES * k, CHUNK_TILES * (k + 1))
+                if j == 2:
+                    floor_tiles(0, 3)
+                    nc.gpsimd.tensor_scalar(
+                        out=cur_fifth[:], in0=cur_sb[:], scalar1=0.2, scalar2=0.0, op0=ALU.mult, op1=ALU.add
+                    )
+                elif j == 3:
+                    floor_tiles(3, 4)
+                    invert_tiles(0, 4)
+                elif j % CHUNK_TILES == 1:
+                    floor_tiles(j - 1, j + 1)
+                    invert_tiles(j - 1, j + 1)
             quantise_chunk(k)
             if k + 1 < CHUNKS:
                 for j in row_tiles(k + 1):
@@ -231,9 +239,9 @@ def tile_ca3_recurrentmatrix_pa_s_kernel(tc, current, memory_matrix, out):
         first_matmul_chunk(CHUNKS - 1)
         scale_half(0)
         turn_back_half(0)
-        regroup(0, 0, N_TILE // 2, nc.vector.tensor_copy)
         scale_half(1)
         turn_back_half(1)
+        regroup(0, 0, N_TILE // 2, nc.vector.tensor_copy)
         for g in range(PASSES):
             max_half(g)
         regroup(1, 0, N_TILE, nc.scalar.copy)

@@ -83,6 +83,7 @@ def tile_ca3_recurrentmatrix_pa_s_kernel(tc, current, memory_matrix, out):
         cur_sumsq = keep.tile([P, 1], F32)
         cur_floor = keep.tile([P, 1], F32)
         cur_inv = keep.tile([P, 1], F32)
+        cur_minus_inv = keep.tile([P, 1], F32)
         simT_sb = keep.tile([P, ROW_TILES, P], F32)
         sim_ps = [sim_psum.tile([P, N_TILE], F32, name="sim_ps%d" % g) for g in range(PASSES)]
         half_max = keep.tile([P, PASSES], F32)
@@ -199,6 +200,9 @@ def tile_ca3_recurrentmatrix_pa_s_kernel(tc, current, memory_matrix, out):
         group_words(cur_bank, cur_grouped[:], nc.vector.tensor_copy)
         floor_squares(cur_sumsq[:], cur_floor[:])
         invert(cur_floor[:], cur_inv[:])
+        nc.gpsimd.tensor_scalar(
+            out=cur_minus_inv[:], in0=cur_inv[:], scalar1=-1.0, scalar2=0.0, op0=ALU.mult, op1=ALU.add
+        )
         turn_tile(0)
         norm_tile(0)
         group_tile(0, nc.vector.tensor_copy)
@@ -210,33 +214,34 @@ def tile_ca3_recurrentmatrix_pa_s_kernel(tc, current, memory_matrix, out):
         turn_tile(1)
         norm_tile(1)
         group_tile(1, nc.vector.tensor_copy)
-        quantise_chunk(0)
         turn_tile(2)
         turn_tile(3)
         keep_warm(sim_ps[1], 1)
         simT_ps = [mx_psum.tile([P, PACK, P], F32, tag="mx", name="simT_ps%d" % g) for g in range(PASSES)]
-        for k in range(1, CHUNKS):
-            for j in row_tiles(k):
-                group_tile(j, nc.vector.tensor_copy)
-                norm_tile(j)
-                if j == 2:
-                    floor_tiles(0, 3)
-                    nc.gpsimd.tensor_scalar(
-                        out=cur_fifth[:], in0=cur_sb[:], scalar1=0.2, scalar2=0.0, op0=ALU.mult, op1=ALU.add
-                    )
-                elif j == 3:
-                    floor_tiles(3, 4)
-                    invert_tiles(0, 4)
-                elif j % CHUNK_TILES == 1:
-                    floor_tiles(j - 1, j + 1)
-                    invert_tiles(j - 1, j + 1)
-            quantise_chunk(k)
-            if k + 1 < CHUNKS:
-                for j in row_tiles(k + 1):
-                    turn_tile(j)
+        for j in range(CHUNK_TILES, ROW_TILES):
+            group_tile(j, nc.vector.tensor_copy)
+            if j in (2, 4):
+                quantise_chunk(j // 2 - 1)
+            norm_tile(j)
+            if j == 2:
+                floor_tiles(0, 3)
+                nc.gpsimd.tensor_scalar(
+                    out=cur_fifth[:], in0=cur_sb[:], scalar1=0.2, scalar2=0.0, op0=ALU.mult, op1=ALU.add
+                )
+            elif j == 3:
+                floor_tiles(3, 4)
+                invert_tiles(0, 4)
+            elif j in (5, 7):
+                floor_tiles(j - 1, j + 1)
+                invert_tiles(j - 1, j + 1)
+            if j + 2 < ROW_TILES:
+                turn_tile(j + 2)
+            if j in (3, 5):
                 keep_warm(sim_ps[1], 1)
-            first_matmul_chunk(k - 1)
-        first_matmul_chunk(CHUNKS - 1)
+                first_matmul_chunk(j // 2 - 1)
+        for k in (2, 3):
+            quantise_chunk(k)
+            first_matmul_chunk(k)
         scale_half(0)
         turn_back_half(0)
         scale_half(1)
@@ -250,11 +255,14 @@ def tile_ca3_recurrentmatrix_pa_s_kernel(tc, current, memory_matrix, out):
         idle_ps = turn_psum.tile([P, N_TILE], F32, tag="turn", name="idle_ps")
         keep_warm(idle_ps, 3)
 
-        row_max = keep.tile([P, 1], F32)
-        nc.vector.reduce_max(out=row_max[:], in_=half_max[:], axis=AXIS_X)
         exp_bias = keep.tile([P, 1], F32)
-        nc.vector.tensor_scalar(
-            out=exp_bias[:], in0=row_max[:], scalar1=cur_inv[:], scalar2=-1.0, op0=ALU.mult, op1=ALU.mult
+        nc.vector.scalar_tensor_tensor(
+            out=exp_bias[:],
+            in0=half_max[:, 0:1],
+            scalar=half_max[:, 1:2],
+            in1=cur_minus_inv[:],
+            op0=ALU.max,
+            op1=ALU.mult,
         )
         e_sb = keep.tile([P, PASSES, N_TILE], BF16)
         e_sum = keep.tile([P, PASSES], F32)
@@ -288,15 +296,14 @@ def tile_ca3_recurrentmatrix_pa_s_kernel(tc, current, memory_matrix, out):
         quantise_regrouped(0, 0)
         quantise_regrouped(1, 0)
         quantise_e(0)
-        quantise_regrouped(1, 1)
-        quantise_e(1)
-
         sum_scaled = keep.tile([P, 1], F32)
         nc.vector.tensor_scalar(
             out=sum_scaled[:], in0=e_sum[:, 0:1], scalar1=e_sum[:, 1:2], scalar2=1.25, op0=ALU.add, op1=ALU.mult
         )
+        quantise_regrouped(1, 1)
         weight = keep.tile([P, 1], F32)
         nc.vector.reciprocal(out=weight[:], in_=sum_scaled[:])
+        quantise_e(1)
 
         keep_warm(idle_ps, 2)
         quantise_regrouped(0, 1)

@@ -26,6 +26,7 @@ N_TILE = 512
 N_TILES = FEATURES // N_TILE
 OUT_TILE = 256
 EPS = 1e-8
+VECTOR_SQUARES = 3
 LOADS = ((0, 1), (1, 2), (2, 4), (4, 6), (6, 8))
 
 FLOPS = 2 * 2 * P * ROWS * FEATURES
@@ -76,7 +77,7 @@ def tile_ca3_recurrentmatrix_pa_s_kernel(tc, current, memory_matrix, out):
 
         cur_fifth = keep.tile([P, FEATURES], F32)
         scalar_squares = keep.tile([P, FEATURES], BF16)
-        cur_squares = keep.tile([P, FEATURES], F32)
+        vector_squares = keep.tile([P, FEATURES], F32)
         mem_sumsq = keep.tile([P, ROW_TILES], F32)
         mem_floor = keep.tile([P, ROW_TILES], F32)
         mem_inv = keep.tile([P, ROW_TILES], F32)
@@ -117,11 +118,25 @@ def tile_ca3_recurrentmatrix_pa_s_kernel(tc, current, memory_matrix, out):
         def group_tile(j, copy):
             group_words(turned[j], memT_grouped[:, j, :, :, :], copy)
 
+        def sum_squares_on_vector(rows_bf16, total):
+            nc.vector.scalar_tensor_tensor(
+                out=vector_squares[:],
+                in0=rows_bf16,
+                scalar=1.0,
+                in1=rows_bf16,
+                op0=ALU.mult,
+                op1=ALU.mult,
+                accum_out=total,
+            )
+
         def norm_tile(j):
             g, t = divmod(j, PACK)
-            nc.scalar.activation(
-                out=scalar_squares[:], in_=mem_sb[:, g, t, :], func=ACT.Square, accum_out=mem_sumsq[:, j : j + 1]
-            )
+            if j == VECTOR_SQUARES:
+                sum_squares_on_vector(mem_sb[:, g, t, :], mem_sumsq[:, j : j + 1])
+            else:
+                nc.scalar.activation(
+                    out=scalar_squares[:], in_=mem_sb[:, g, t, :], func=ACT.Square, accum_out=mem_sumsq[:, j : j + 1]
+                )
 
         def floor_tiles(first, last):
             floor_squares(mem_sumsq[:, first:last], mem_floor[:, first:last])
@@ -151,18 +166,19 @@ def tile_ca3_recurrentmatrix_pa_s_kernel(tc, current, memory_matrix, out):
                         stop=(q == PASSES - 1),
                     )
 
-        def scale_half(g):
-            tiles = slice(PACK * g, PACK * (g + 1))
+        def scale(first, last):
+            g, t0 = divmod(first, PACK)
             nc.vector.tensor_tensor(
-                out=simT_sb[:, tiles, :],
-                in0=simT_ps[g][:],
-                in1=mem_inv[:, tiles].unsqueeze(2).to_broadcast([P, PACK, P]),
+                out=simT_sb[:, first:last, :],
+                in0=simT_ps[g][:, t0 : t0 + last - first, :],
+                in1=mem_inv[:, first:last].unsqueeze(2).to_broadcast([P, last - first, P]),
                 op=ALU.mult,
             )
 
-        def turn_back_half(g):
-            for t in range(PACK):
-                nc.tensor.transpose(sim_ps[g][:, t * P : (t + 1) * P], simT_sb[:, PACK * g + t, :], ident_f32[:])
+        def turn_back(first, last):
+            for j in range(first, last):
+                g, t = divmod(j, PACK)
+                nc.tensor.transpose(sim_ps[g][:, t * P : (t + 1) * P], simT_sb[:, j, :], ident_f32[:])
 
         def max_half(g):
             nc.vector.reduce_max(out=half_max[:, g : g + 1], in_=sim_ps[g][:], axis=AXIS_X)
@@ -174,8 +190,8 @@ def tile_ca3_recurrentmatrix_pa_s_kernel(tc, current, memory_matrix, out):
                 in_=mem_sb[:, g, :, cols].rearrange("p t (c i) -> p c t i", i=4),
             )
 
-        def quantise_regrouped(g, n):
-            cols = slice(n * N_TILE, (n + 1) * N_TILE)
+        def quantise_regrouped(g, first, last):
+            cols = slice(first, last)
             nc.vector.quantize_mx(
                 out=mem_codes[:, g, cols].bitcast(FP8X4),
                 scales=mem_scales[:, g, cols],
@@ -188,15 +204,7 @@ def tile_ca3_recurrentmatrix_pa_s_kernel(tc, current, memory_matrix, out):
 
         keep_warm(sim_ps[1], 2)
         cur_bank = turn_words(cur_sb[:])
-        nc.vector.scalar_tensor_tensor(
-            out=cur_squares[:],
-            in0=cur_sb[:],
-            scalar=1.0,
-            in1=cur_sb[:],
-            op0=ALU.mult,
-            op1=ALU.mult,
-            accum_out=cur_sumsq[:],
-        )
+        sum_squares_on_vector(cur_sb[:], cur_sumsq[:])
         group_words(cur_bank, cur_grouped[:], nc.vector.tensor_copy)
         floor_squares(cur_sumsq[:], cur_floor[:])
         invert(cur_floor[:], cur_inv[:])
@@ -214,6 +222,7 @@ def tile_ca3_recurrentmatrix_pa_s_kernel(tc, current, memory_matrix, out):
         turn_tile(1)
         norm_tile(1)
         group_tile(1, nc.vector.tensor_copy)
+        norm_tile(VECTOR_SQUARES)
         turn_tile(2)
         turn_tile(3)
         keep_warm(sim_ps[1], 1)
@@ -222,7 +231,8 @@ def tile_ca3_recurrentmatrix_pa_s_kernel(tc, current, memory_matrix, out):
             group_tile(j, nc.vector.tensor_copy)
             if j in (2, 4):
                 quantise_chunk(j // 2 - 1)
-            norm_tile(j)
+            if j != VECTOR_SQUARES:
+                norm_tile(j)
             if j == 2:
                 floor_tiles(0, 3)
                 nc.gpsimd.tensor_scalar(
@@ -239,14 +249,22 @@ def tile_ca3_recurrentmatrix_pa_s_kernel(tc, current, memory_matrix, out):
             if j in (3, 5):
                 keep_warm(sim_ps[1], 1)
                 first_matmul_chunk(j // 2 - 1)
+        for first in (0, N_TILE // 2):
+            cols = slice(first, first + N_TILE // 2)
+            nc.gpsimd.tensor_scalar(
+                out=mem_grouped[:, 0, cols, :],
+                in0=mem_sb[:, 0, :, cols].rearrange("p t d -> p d t"),
+                scalar1=1.0,
+                scalar2=0.0,
+                op0=ALU.mult,
+                op1=ALU.add,
+            )
         for k in (2, 3):
             quantise_chunk(k)
             first_matmul_chunk(k)
-        scale_half(0)
-        turn_back_half(0)
-        scale_half(1)
-        turn_back_half(1)
-        regroup(0, 0, N_TILE // 2, nc.vector.tensor_copy)
+        for first, last in ((0, 4), (4, 6), (6, 8)):
+            scale(first, last)
+            turn_back(first, last)
         for g in range(PASSES):
             max_half(g)
         regroup(1, 0, N_TILE, nc.scalar.copy)
@@ -256,11 +274,11 @@ def tile_ca3_recurrentmatrix_pa_s_kernel(tc, current, memory_matrix, out):
         keep_warm(idle_ps, 3)
 
         exp_bias = keep.tile([P, 1], F32)
-        nc.vector.scalar_tensor_tensor(
+        nc.vector.tensor_scalar(
             out=exp_bias[:],
             in0=half_max[:, 0:1],
-            scalar=half_max[:, 1:2],
-            in1=cur_minus_inv[:],
+            scalar1=half_max[:, 1:2],
+            scalar2=cur_minus_inv[:],
             op0=ALU.max,
             op1=ALU.mult,
         )
@@ -283,7 +301,6 @@ def tile_ca3_recurrentmatrix_pa_s_kernel(tc, current, memory_matrix, out):
         for g in range(PASSES):
             nc.scalar.copy(out=e_grouped[:, g, :, :].bitcast(F32), in_=eT_ps[g][:].rearrange("p u b -> p b u"))
         regroup(0, FEATURES - N_TILE // 2, FEATURES, nc.scalar.copy)
-        regroup(0, N_TILE // 2, N_TILE, nc.vector.tensor_copy)
         regroup(0, N_TILE, FEATURES - N_TILE // 2, nc.vector.tensor_copy)
 
         def quantise_e(g):
@@ -293,20 +310,20 @@ def tile_ca3_recurrentmatrix_pa_s_kernel(tc, current, memory_matrix, out):
                 in_=e_grouped[:, g, :, :].rearrange("p b t -> p (b t)"),
             )
 
-        quantise_regrouped(0, 0)
-        quantise_regrouped(1, 0)
+        quantise_regrouped(1, 0, N_TILE)
+        quantise_regrouped(0, 0, N_TILE)
         quantise_e(0)
         sum_scaled = keep.tile([P, 1], F32)
         nc.vector.tensor_scalar(
             out=sum_scaled[:], in0=e_sum[:, 0:1], scalar1=e_sum[:, 1:2], scalar2=1.25, op0=ALU.add, op1=ALU.mult
         )
-        quantise_regrouped(1, 1)
+        quantise_regrouped(1, N_TILE, FEATURES)
         weight = keep.tile([P, 1], F32)
         nc.vector.reciprocal(out=weight[:], in_=sum_scaled[:])
         quantise_e(1)
+        quantise_regrouped(0, N_TILE, FEATURES - N_TILE // 2)
 
-        keep_warm(idle_ps, 2)
-        quantise_regrouped(0, 1)
+        quantise_regrouped(0, FEATURES - N_TILE // 2, FEATURES)
         attracted = [mx_psum.tile([P, N_TILE], F32, tag="mx", name="attracted%d" % n) for n in range(N_TILES)]
         for n, g, start, stop in ((0, 0, True, False), (0, 1, False, True), (1, 1, True, False), (1, 0, False, True)):
             cols = slice(n * N_TILE, (n + 1) * N_TILE)

@@ -19,8 +19,6 @@ PACK = 4
 K_PASS = P * PACK
 PASSES = 2
 ROW_TILES = ROWS // P
-CHUNK_TILES = 2
-CHUNKS = ROW_TILES // CHUNK_TILES
 WORD_BLOCKS = FEATURES // 2 // P
 N_TILE = 512
 N_TILES = FEATURES // N_TILE
@@ -54,7 +52,7 @@ def tile_ca3_recurrentmatrix_pa_s_kernel(tc, current, memory_matrix, out):
 
         ident_f32 = keep.tile([P, P], F32)
         make_identity(nc, ident_f32[:])
-        minus_half = keep.tile([P, PACK], F32)
+        minus_half = keep.tile([P, ROW_TILES], F32)
         nc.gpsimd.memset(minus_half[:], -0.5)
 
         zero = keep.tile([P, 1], F32)
@@ -108,9 +106,6 @@ def tile_ca3_recurrentmatrix_pa_s_kernel(tc, current, memory_matrix, out):
                 out=inverse, in0=floored, in1=minus_half[:, 0 : floored.shape[1]], op=ALU.pow
             )
 
-        def row_tiles(k):
-            return range(CHUNK_TILES * k, CHUNK_TILES * (k + 1))
-
         def turn_tile(j):
             g, t = divmod(j, PACK)
             turned[j] = turn_words(mem_sb[:, g, t, :])
@@ -144,16 +139,15 @@ def tile_ca3_recurrentmatrix_pa_s_kernel(tc, current, memory_matrix, out):
         def invert_tiles(first, last):
             invert(mem_floor[:, first:last], mem_inv[:, first:last])
 
-        def quantise_chunk(k):
-            tiles = slice(CHUNK_TILES * k, CHUNK_TILES * (k + 1))
+        def quantise(first, last):
             nc.vector.quantize_mx(
-                out=memT_codes[:, tiles, :, :].rearrange("p j q c -> p (j q c)").bitcast(FP8X4),
-                scales=memT_scales[:, tiles, :, :].rearrange("p j q c -> p (j q c)"),
-                in_=memT_grouped[:, tiles, :, :, :].rearrange("p j q c t -> p (j q c t)"),
+                out=memT_codes[:, first:last, :, :].rearrange("p j q c -> p (j q c)").bitcast(FP8X4),
+                scales=memT_scales[:, first:last, :, :].rearrange("p j q c -> p (j q c)"),
+                in_=memT_grouped[:, first:last, :, :, :].rearrange("p j q c t -> p (j q c t)"),
             )
 
-        def first_matmul_chunk(k):
-            for j in row_tiles(k):
+        def first_matmul(first, last):
+            for j in range(first, last):
                 g, t = divmod(j, PACK)
                 for q in range(PASSES):
                     nc.tensor.matmul_mx(
@@ -227,10 +221,10 @@ def tile_ca3_recurrentmatrix_pa_s_kernel(tc, current, memory_matrix, out):
         turn_tile(3)
         keep_warm(sim_ps[1], 1)
         simT_ps = [mx_psum.tile([P, PACK, P], F32, tag="mx", name="simT_ps%d" % g) for g in range(PASSES)]
-        for j in range(CHUNK_TILES, ROW_TILES):
+        for j in range(2, ROW_TILES):
             group_tile(j, nc.vector.tensor_copy)
-            if j in (2, 4):
-                quantise_chunk(j // 2 - 1)
+            if j == 4:
+                quantise(0, 4)
             if j != VECTOR_SQUARES:
                 norm_tile(j)
             if j == 2:
@@ -238,17 +232,17 @@ def tile_ca3_recurrentmatrix_pa_s_kernel(tc, current, memory_matrix, out):
                 nc.gpsimd.tensor_scalar(
                     out=cur_fifth[:], in0=cur_sb[:], scalar1=0.2, scalar2=0.0, op0=ALU.mult, op1=ALU.add
                 )
-            elif j == 3:
-                floor_tiles(3, 4)
-                invert_tiles(0, 4)
-            elif j in (5, 7):
-                floor_tiles(j - 1, j + 1)
-                invert_tiles(j - 1, j + 1)
+            elif j == 5:
+                floor_tiles(3, 6)
+                invert_tiles(0, 6)
+            elif j == 7:
+                floor_tiles(6, 8)
+                invert_tiles(6, 8)
             if j + 2 < ROW_TILES:
                 turn_tile(j + 2)
-            if j in (3, 5):
-                keep_warm(sim_ps[1], 1)
-                first_matmul_chunk(j // 2 - 1)
+            if j == 5:
+                keep_warm(sim_ps[1], 2)
+                first_matmul(0, 4)
         for first in (0, N_TILE // 2):
             cols = slice(first, first + N_TILE // 2)
             nc.gpsimd.tensor_scalar(
@@ -259,9 +253,9 @@ def tile_ca3_recurrentmatrix_pa_s_kernel(tc, current, memory_matrix, out):
                 op0=ALU.mult,
                 op1=ALU.add,
             )
-        for k in (2, 3):
-            quantise_chunk(k)
-            first_matmul_chunk(k)
+        for first, last in ((4, 6), (6, 8)):
+            quantise(first, last)
+            first_matmul(first, last)
         for first, last in ((0, 4), (4, 6), (6, 8)):
             scale(first, last)
             turn_back(first, last)

from contextlib import ExitStack

import concourse.mybir as mybir
from concourse.masks import make_identity

F32 = mybir.dt.float32
BF16 = mybir.dt.bfloat16
U32 = mybir.dt.uint32
U8 = mybir.dt.uint8
FP8X4 = mybir.dt.float8_e4m3fn_x4
ACT = mybir.ActivationFunctionType
ALU = mybir.AluOpType
AXIS_X = mybir.AxisListType.X

P = 128
ROWS = 1024
FEATURES = 1024
PACK = 4
K_PASS = P * PACK
PASSES = 2
ROW_TILES = ROWS // P
WORD_BLOCKS = FEATURES // 2 // P
N_TILE = 512
N_TILES = FEATURES // N_TILE
OUT_TILE = 256
EPS = 1e-8
VECTOR_SQUARES = 3
LOADS = ((0, 1), (1, 2), (2, 4), (4, 6), (6, 8))

FLOPS = 2 * 2 * P * ROWS * FEATURES


def tile_ca3_recurrentmatrix_pa_s_kernel(tc, current, memory_matrix, out):
    nc = tc.nc
    with ExitStack() as ctx:
        keep = ctx.enter_context(tc.tile_pool(name="keep", bufs=1))
        turn_psum = ctx.enter_context(tc.psum_pool(name="turn_psum", bufs=4))
        mx_psum = ctx.enter_context(tc.psum_pool(name="mx_psum", bufs=2))
        sim_psum = ctx.enter_context(tc.psum_pool(name="sim_psum", bufs=1))
        ctx.enter_context(tc.manual_schedule())

        cur_sb = keep.tile([P, FEATURES], BF16)
        nc.sync.dma_start(out=cur_sb[:], in_=current)
        mem_sb = keep.tile([P, PASSES, PACK, FEATURES], BF16)
        mem_rows = memory_matrix.rearrange("(g p t) d -> p g t d", g=PASSES, t=PACK)
        for first, last in LOADS:
            g, t0 = divmod(first, PACK)
            nc.sync.dma_start(
                out=mem_sb[:, g, t0 : t0 + last - first, :],
                in_=mem_rows[:, g, t0 : t0 + last - first, :],
            )

        ident_f32 = keep.tile([P, P], F32)
        make_identity(nc, ident_f32[:])
        minus_half = keep.tile([P, ROW_TILES], F32)
        nc.gpsimd.memset(minus_half[:], -0.5)

        zero = keep.tile([P, 1], F32)
        nc.vector.memset(zero[:], 0.0)
        warm_exp = keep.tile([P, 1], F32)
        nc.scalar.activation(out=warm_exp[:], in_=zero[:], func=ACT.Exp)

        cur_grouped = keep.tile([P, PASSES, P, PACK], BF16, align_bytes=64)
        cur_codes = keep.tile([P, PASSES, P], U32, align_bytes=64)
        cur_scales = keep.tile([P, PASSES, P], U8, align_bytes=64)
        memT_grouped = keep.tile([P, ROW_TILES, PASSES, P, PACK], BF16, align_bytes=64)
        memT_codes = keep.tile([P, ROW_TILES, PASSES, P], U32, align_bytes=64)
        memT_scales = keep.tile([P, ROW_TILES, PASSES, P], U8, align_bytes=64)
        mem_grouped = keep.tile([P, PASSES, FEATURES, PACK], BF16, align_bytes=64)
        mem_codes = keep.tile([P, PASSES, FEATURES], U32, align_bytes=64)
        mem_scales = keep.tile([P, PASSES, FEATURES], U8, align_bytes=64)
        e_grouped = keep.tile([P, PASSES, P, PACK], BF16, align_bytes=64)
        e_codes = keep.tile([P, PASSES, P], U32, align_bytes=64)
        e_scales = keep.tile([P, PASSES, P], U8, align_bytes=64)

        cur_fifth = keep.tile([P, FEATURES], F32)
        scalar_squares = keep.tile([P, FEATURES], BF16)
        vector_squares = keep.tile([P, FEATURES], F32)
        mem_sumsq = keep.tile([P, ROW_TILES], F32)
        mem_floor = keep.tile([P, ROW_TILES], F32)
        mem_inv = keep.tile([P, ROW_TILES], F32)
        cur_sumsq = keep.tile([P, 1], F32)
        cur_floor = keep.tile([P, 1], F32)
        cur_inv = keep.tile([P, 1], F32)
        cur_minus_inv = keep.tile([P, 1], F32)
        simT_sb = keep.tile([P, ROW_TILES, P], F32)
        sim_ps = [sim_psum.tile([P, N_TILE], F32, name="sim_ps%d" % g) for g in range(PASSES)]
        half_max = keep.tile([P, PASSES], F32)
        turned = {}

        def turn_words(rows_bf16):
            words = rows_bf16.bitcast(F32)
            bank = turn_psum.tile([P, WORD_BLOCKS, P], F32, tag="turn")
            for w in range(WORD_BLOCKS):
                nc.tensor.transpose(bank[:, w, :], words[:, w * P : (w + 1) * P], ident_f32[:])
            return bank

        def group_words(bank, grouped, copy):
            copy(out=grouped.bitcast(F32), in_=bank[:].rearrange("p (q u) r -> p q r u", u=2))

        def floor_squares(sumsq, floored):
            nc.gpsimd.tensor_scalar_max(out=floored, in0=sumsq, scalar1=EPS * EPS)

        def invert(floored, inverse):
            nc.gpsimd.tensor_tensor(
                out=inverse, in0=floored, in1=minus_half[:, 0 : floored.shape[1]], op=ALU.pow
            )

        def turn_tile(j):
            g, t = divmod(j, PACK)
            turned[j] = turn_words(mem_sb[:, g, t, :])

        def group_tile(j, copy):
            group_words(turned[j], memT_grouped[:, j, :, :, :], copy)

        def sum_squares_on_vector(rows_bf16, total):
            nc.vector.scalar_tensor_tensor(
                out=vector_squares[:],
                in0=rows_bf16,
                scalar=1.0,
                in1=rows_bf16,
                op0=ALU.mult,
                op1=ALU.mult,
                accum_out=total,
            )

        def norm_tile(j):
            g, t = divmod(j, PACK)
            if j == VECTOR_SQUARES:
                sum_squares_on_vector(mem_sb[:, g, t, :], mem_sumsq[:, j : j + 1])
            else:
                nc.scalar.activation(
                    out=scalar_squares[:], in_=mem_sb[:, g, t, :], func=ACT.Square, accum_out=mem_sumsq[:, j : j + 1]
                )

        def floor_tiles(first, last):
            floor_squares(mem_sumsq[:, first:last], mem_floor[:, first:last])

        def invert_tiles(first, last):
            invert(mem_floor[:, first:last], mem_inv[:, first:last])

        def quantise(first, last):
            nc.vector.quantize_mx(
                out=memT_codes[:, first:last, :, :].rearrange("p j q c -> p (j q c)").bitcast(FP8X4),
                scales=memT_scales[:, first:last, :, :].rearrange("p j q c -> p (j q c)"),
                in_=memT_grouped[:, first:last, :, :, :].rearrange("p j q c t -> p (j q c t)"),
            )

        def first_matmul(first, last):
            for j in range(first, last):
                g, t = divmod(j, PACK)
                for q in range(PASSES):
                    nc.tensor.matmul_mx(
                        out=simT_ps[g][:, t, :],
                        lhsT=memT_codes[:, j, q, :].bitcast(FP8X4),
                        lhsT_scale=memT_scales[:, j, q, :],
                        rhs=cur_codes[:, q, :].bitcast(FP8X4),
                        rhs_scale=cur_scales[:, q, :],
                        start=(q == 0),
                        stop=(q == PASSES - 1),
                    )

        def scale(first, last):
            g, t0 = divmod(first, PACK)
            nc.vector.tensor_tensor(
                out=simT_sb[:, first:last, :],
                in0=simT_ps[g][:, t0 : t0 + last - first, :],
                in1=mem_inv[:, first:last].unsqueeze(2).to_broadcast([P, last - first, P]),
                op=ALU.mult,
            )

        def turn_back(first, last):
            for j in range(first, last):
                g, t = divmod(j, PACK)
                nc.tensor.transpose(sim_ps[g][:, t * P : (t + 1) * P], simT_sb[:, j, :], ident_f32[:])

        def max_half(g):
            nc.vector.reduce_max(out=half_max[:, g : g + 1], in_=sim_ps[g][:], axis=AXIS_X)

        def regroup(g, first, last, copy):
            cols = slice(first, last)
            copy(
                out=mem_grouped[:, g, cols, :].rearrange("p (c i) t -> p c t i", i=4),
                in_=mem_sb[:, g, :, cols].rearrange("p t (c i) -> p c t i", i=4),
            )

        def quantise_regrouped(g, first, last):
            cols = slice(first, last)
            nc.vector.quantize_mx(
                out=mem_codes[:, g, cols].bitcast(FP8X4),
                scales=mem_scales[:, g, cols],
                in_=mem_grouped[:, g, cols, :].rearrange("p d t -> p (d t)"),
            )

        def keep_warm(bank, count):
            for i in range(count):
                nc.tensor.matmul(bank[:, 0:P], lhsT=ident_f32[:], rhs=ident_f32[:], start=True, stop=True)

        keep_warm(sim_ps[1], 2)
        cur_bank = turn_words(cur_sb[:])
        sum_squares_on_vector(cur_sb[:], cur_sumsq[:])
        group_words(cur_bank, cur_grouped[:], nc.vector.tensor_copy)
        floor_squares(cur_sumsq[:], cur_floor[:])
        invert(cur_floor[:], cur_inv[:])
        nc.gpsimd.tensor_scalar(
            out=cur_minus_inv[:], in0=cur_inv[:], scalar1=-1.0, scalar2=0.0, op0=ALU.mult, op1=ALU.add
        )
        turn_tile(0)
        norm_tile(0)
        group_tile(0, nc.vector.tensor_copy)
        nc.vector.quantize_mx(
            out=cur_codes[:].rearrange("p q b -> p (q b)").bitcast(FP8X4),
            scales=cur_scales[:].rearrange("p q b -> p (q b)"),
            in_=cur_grouped[:].rearrange("p q b t -> p (q b t)"),
        )
        turn_tile(1)
        norm_tile(1)
        group_tile(1, nc.vector.tensor_copy)
        norm_tile(VECTOR_SQUARES)
        turn_tile(2)
        turn_tile(3)
        keep_warm(sim_ps[1], 1)
        simT_ps = [mx_psum.tile([P, PACK, P], F32, tag="mx", name="simT_ps%d" % g) for g in range(PASSES)]
        for j in range(2, ROW_TILES):
            group_tile(j, nc.vector.tensor_copy)
            if j == 4:
                quantise(0, 4)
            if j != VECTOR_SQUARES:
                norm_tile(j)
            if j == 2:
                floor_tiles(0, 3)
                nc.gpsimd.tensor_scalar(
                    out=cur_fifth[:], in0=cur_sb[:], scalar1=0.2, scalar2=0.0, op0=ALU.mult, op1=ALU.add
                )
            elif j == 5:
                floor_tiles(3, 6)
                invert_tiles(0, 6)
            elif j == 7:
                floor_tiles(6, 8)
                invert_tiles(6, 8)
            if j + 2 < ROW_TILES:
                turn_tile(j + 2)
            if j == 5:
                keep_warm(sim_ps[1], 2)
                first_matmul(0, 4)
        for first in (0, N_TILE // 2):
            cols = slice(first, first + N_TILE // 2)
            nc.gpsimd.tensor_scalar(
                out=mem_grouped[:, 0, cols, :],
                in0=mem_sb[:, 0, :, cols].rearrange("p t d -> p d t"),
                scalar1=1.0,
                scalar2=0.0,
                op0=ALU.mult,
                op1=ALU.add,
            )
        for first, last in ((4, 6), (6, 8)):
            quantise(first, last)
            first_matmul(first, last)
        for first, last in ((0, 4), (4, 6), (6, 8)):
            scale(first, last)
            turn_back(first, last)
        for g in range(PASSES):
            max_half(g)
        regroup(1, 0, N_TILE, nc.scalar.copy)
        regroup(1, N_TILE, FEATURES, nc.scalar.copy)

        idle_ps = turn_psum.tile([P, N_TILE], F32, tag="turn", name="idle_ps")
        keep_warm(idle_ps, 3)

        exp_bias = keep.tile([P, 1], F32)
        nc.vector.tensor_scalar(
            out=exp_bias[:],
            in0=half_max[:, 0:1],
            scalar1=half_max[:, 1:2],
            scalar2=cur_minus_inv[:],
            op0=ALU.max,
            op1=ALU.mult,
        )
        e_sb = keep.tile([P, PASSES, N_TILE], BF16)
        e_sum = keep.tile([P, PASSES], F32)
        eT_ps = {}
        for g in range(PASSES):
            nc.scalar.activation(
                out=e_sb[:, g, :].rearrange("b (u p i) -> b u p i", u=2, i=2),
                in_=sim_ps[g][:].rearrange("b (u i p) -> b u p i", u=2, i=2),
                func=ACT.Exp,
                bias=exp_bias[:],
                scale=cur_inv[:],
                accum_out=e_sum[:, g : g + 1],
            )
            eT_ps[g] = turn_psum.tile([P, 2, P], F32, tag="turn", name="eT_ps%d" % g)
            words = e_sb[:, g, :].bitcast(F32)
            for u in range(2):
                nc.tensor.transpose(eT_ps[g][:, u, :], words[:, u * P : (u + 1) * P], ident_f32[:])
        for g in range(PASSES):
            nc.scalar.copy(out=e_grouped[:, g, :, :].bitcast(F32), in_=eT_ps[g][:].rearrange("p u b -> p b u"))
        regroup(0, FEATURES - N_TILE // 2, FEATURES, nc.scalar.copy)
        regroup(0, N_TILE, FEATURES - N_TILE // 2, nc.vector.tensor_copy)

        def quantise_e(g):
            nc.vector.quantize_mx(
                out=e_codes[:, g, :].bitcast(FP8X4),
                scales=e_scales[:, g, :],
                in_=e_grouped[:, g, :, :].rearrange("p b t -> p (b t)"),
            )

        quantise_regrouped(1, 0, N_TILE)
        quantise_regrouped(0, 0, N_TILE)
        quantise_e(0)
        sum_scaled = keep.tile([P, 1], F32)
        nc.vector.tensor_scalar(
            out=sum_scaled[:], in0=e_sum[:, 0:1], scalar1=e_sum[:, 1:2], scalar2=1.25, op0=ALU.add, op1=ALU.mult
        )
        quantise_regrouped(1, N_TILE, FEATURES)
        weight = keep.tile([P, 1], F32)
        nc.vector.reciprocal(out=weight[:], in_=sum_scaled[:])
        quantise_e(1)
        quantise_regrouped(0, N_TILE, FEATURES - N_TILE // 2)

        quantise_regrouped(0, FEATURES - N_TILE // 2, FEATURES)
        attracted = [mx_psum.tile([P, N_TILE], F32, tag="mx", name="attracted%d" % n) for n in range(N_TILES)]
        for n, g, start, stop in ((0, 0, True, False), (0, 1, False, True), (1, 1, True, False), (1, 0, False, True)):
            cols = slice(n * N_TILE, (n + 1) * N_TILE)
            nc.tensor.matmul_mx(
                out=attracted[n][:],
                lhsT=e_codes[:, g, :].bitcast(FP8X4),
                lhsT_scale=e_scales[:, g, :],
                rhs=mem_codes[:, g, cols].bitcast(FP8X4),
                rhs_scale=mem_scales[:, g, cols],
                start=start,
                stop=stop,
            )
        out_sb = keep.tile([P, FEATURES], F32)
        for first in range(0, FEATURES, OUT_TILE):
            cols = slice(first, first + OUT_TILE)
            n, offset = divmod(first, N_TILE)
            nc.vector.scalar_tensor_tensor(
                out=out_sb[:, cols],
                in0=attracted[n][:, offset : offset + OUT_TILE],
                scalar=weight[:],
                in1=cur_fifth[:, cols],
                op0=ALU.mult,
                op1=ALU.add,
            )
            nc.sync.dma_start(out=out[:, cols], in_=out_sb[:, cols])
